import numpy as np
import ml_dtypes

BF16 = ml_dtypes.bfloat16


def bf(x):
    return np.asarray(x, np.float32).astype(BF16)


def f32(x):
    return np.asarray(x, np.float32)


def f64(x):
    return np.asarray(x).astype(np.float64)


def striped(idx):
    return np.tile(idx.reshape(-1, 16).T, (8, 1))


S, D, H1, H2, N = 4096, 128, 256, 128, 2048


def xavier(fan_in, fan_out):
    lim = np.sqrt(6.0 / (fan_in + fan_out))
    return np.random.uniform(-lim, lim, (fan_in, fan_out))


def setup_inputs():
    return {"table": bf(np.random.standard_normal((D, S))), "w1": bf(xavier(D, H1)), "adj_t": bf(np.random.uniform(-1.0, 1.0, (N, N)) * np.sqrt(3.0 / N)), "wm": bf(xavier(H1, H2)), "ws": bf(0.5 * xavier(H1, H2)), "wp": bf(xavier(H2, H2)), "bp": f32(0.1 * np.random.standard_normal((H2, 1))), "noise": f32(np.random.standard_normal((H2, N))), "offs": striped(np.random.permutation(S)[:N])}


def reference(table, w1, adj_t, wm, ws, wp, bp, noise, offs):
    idx = offs[:16].T.reshape(-1)
    a = f64(adj_t)
    xw = f64(w1).T @ f64(table)[:, idx]
    hidden = np.maximum(xw @ a, 0.0)
    z = (f64(wm).T @ hidden) @ a
    mean = f64(wp).T @ z + f64(bp)
    logstd = (f64(ws).T @ hidden) @ a
    return f64(noise) * np.exp(logstd) + mean

@@ -1,0 +1,165 @@
+import concourse.mybir as mybir
+from concourse.masks import make_identity
+
+BF16, F32, U16 = mybir.dt.bfloat16, mybir.dt.float32, mybir.dt.uint16
+FUNC = mybir.ActivationFunctionType
+ALU = mybir.AluOpType
+
+P = 128
+S = 4096
+N = 2048
+H1, H2 = 256, 128
+PIECE = 512
+N_PIECES = N // PIECE
+N_BLOCKS = N // P
+BLOCKS_PER_PIECE = PIECE // P
+H1_HALVES = H1 // P
+OFFSET_COLS = PIECE // 16
+
+FLOPS = 2 * (P * H1 * N + H1 * N * N + 2 * H1 * H2 * N + 2 * H2 * N * N + H2 * H2 * N)
+
+
+def tile_vgae_encoder_b_kernel(tc, table, w1, adj_t, wm, ws, wp, bp, noise, offs, out):
+    nc = tc.nc
+    with (
+        tc.tile_pool(name="held", bufs=1) as held,
+        tc.tile_pool(name="work", bufs=2) as work,
+        tc.psum_pool(name="banks", bufs=4) as banks,
+        tc.psum_pool(name="flipped", bufs=2) as flipped,
+        tc.psum_pool(name="projected", bufs=2) as projected,
+    ):
+        offsets = held.tile([P, N // 16], U16, name="offsets")
+        nc.sync.dma_start(offsets[:], offs)
+        table_sb = held.tile([P, S], BF16, name="table_sb")
+        nc.sync.dma_start(table_sb[:], table)
+        w1_sb = held.tile([P, H1], BF16, name="w1_sb")
+        nc.scalar.dma_start(w1_sb[:], w1)
+
+        adj_blocks = adj_t.rearrange("(b p) i -> p b i", p=P)
+        adj_sb = []
+        for piece in range(N_PIECES):
+            cols = slice(piece * PIECE, (piece + 1) * PIECE)
+            row = []
+            for g in range(N_BLOCKS // BLOCKS_PER_PIECE):
+                part = held.tile([P, BLOCKS_PER_PIECE, PIECE], BF16, name=f"adj_{piece}_{g}")
+                nc.sync.dma_start(
+                    part[:], adj_blocks[:, g * BLOCKS_PER_PIECE : (g + 1) * BLOCKS_PER_PIECE, cols]
+                )
+                row.append(part)
+            adj_sb.append(row)
+            if piece == 0:
+                wms_sb = held.tile([P, H1_HALVES, 2 * H2], BF16, name="wms_sb")
+                nc.sync.dma_start(wms_sb[:, :, 0:H2], wm.rearrange("(h p) c -> p h c", p=P))
+                nc.sync.dma_start(wms_sb[:, :, H2 : 2 * H2], ws.rearrange("(h p) c -> p h c", p=P))
+                wp_sb = held.tile([P, H2], BF16, name="wp_sb")
+                nc.sync.dma_start(wp_sb[:], wp)
+                bp_sb = held.tile([P, 1], F32, name="bp_sb")
+                nc.sync.dma_start(bp_sb[:], bp)
+        noise_sb = held.tile([P, N], F32, name="noise_sb")
+        nc.sync.dma_start(noise_sb[:], noise)
+
+        def adj(block, piece):
+            return adj_sb[piece][block // BLOCKS_PER_PIECE][:, block % BLOCKS_PER_PIECE, :]
+
+        identity = held.tile([P, P], BF16, name="identity")
+        make_identity(nc, identity[:])
+
+        xw_sb = [held.tile([P, N], BF16, name=f"xw_sb{h}") for h in range(H1_HALVES)]
+        for piece in range(N_PIECES):
+            cols = slice(piece * PIECE, (piece + 1) * PIECE)
+            piece_offsets = offsets[:, piece * OFFSET_COLS : (piece + 1) * OFFSET_COLS]
+            for h in range(H1_HALVES):
+                xw_ps = banks.tile([P, PIECE], F32, name="xw_ps", tag="bank")
+                nc.tensor.matmul(
+                    xw_ps[:],
+                    w1_sb[:, h * P : (h + 1) * P],
+                    table_sb[:].indirect(piece_offsets),
+                    start=True,
+                    stop=True,
+                )
+                if h == 0:
+                    nc.scalar.activation(xw_sb[h][:, cols], xw_ps[:], FUNC.Copy)
+                else:
+                    nc.vector.tensor_copy(xw_sb[h][:, cols], xw_ps[:])
+
+        xwT_sb = held.tile([P, N_BLOCKS, H1], BF16, name="xwT_sb")
+        for piece in range(N_PIECES):
+            xwT_ps = flipped.tile([P, BLOCKS_PER_PIECE, H1], BF16, name="xwT_ps")
+            for k in range(BLOCKS_PER_PIECE):
+                block = piece * BLOCKS_PER_PIECE + k
+                for h in range(H1_HALVES):
+                    nc.tensor.transpose(
+                        xwT_ps[:, k, h * P : (h + 1) * P],
+                        xw_sb[h][:, block * P : (block + 1) * P],
+                        identity[:],
+                    )
+            nc.vector.tensor_copy(
+                xwT_sb[:, piece * BLOCKS_PER_PIECE : (piece + 1) * BLOCKS_PER_PIECE, :], xwT_ps[:]
+            )
+
+        hidden_sb = [held.tile([P, N], BF16, name=f"hidden_sb{h}") for h in range(H1_HALVES)]
+        tmsT_sb = held.tile([P, N_BLOCKS, 2 * H2], BF16, name="tmsT_sb")
+        for piece in range(N_PIECES):
+            cols = slice(piece * PIECE, (piece + 1) * PIECE)
+            for h in range(H1_HALVES):
+                hidden_ps = banks.tile([P, PIECE], F32, name="hidden_ps", tag="bank")
+                for block in range(N_BLOCKS):
+                    nc.tensor.matmul(
+                        hidden_ps[:],
+                        xwT_sb[:, block, h * P : (h + 1) * P],
+                        adj(block, piece),
+                        start=(block == 0),
+                        stop=(block == N_BLOCKS - 1),
+                    )
+                if h == 0:
+                    nc.scalar.activation(hidden_sb[h][:, cols], hidden_ps[:], FUNC.Relu)
+                else:
+                    nc.vector.tensor_scalar_max(hidden_sb[h][:, cols], hidden_ps[:], 0.0)
+            for k in range(BLOCKS_PER_PIECE):
+                block = piece * BLOCKS_PER_PIECE + k
+                tmsT_ps = projected.tile([P, 2 * H2], F32, name="tmsT_ps")
+                for h in range(H1_HALVES):
+                    nc.tensor.matmul(
+                        tmsT_ps[:],
+                        hidden_sb[h][:, block * P : (block + 1) * P],
+                        wms_sb[:, h, :],
+                        start=(h == 0),
+                        stop=(h == H1_HALVES - 1),
+                    )
+                nc.vector.tensor_copy(tmsT_sb[:, block, :], tmsT_ps[:])
+
+        for piece in range(N_PIECES):
+            cols = slice(piece * PIECE, (piece + 1) * PIECE)
+            z_ps = banks.tile([P, PIECE], F32, name="z_ps", tag="bank")
+            for block in range(N_BLOCKS):
+                nc.tensor.matmul(
+                    z_ps[:],
+                    tmsT_sb[:, block, 0:H2],
+                    adj(block, piece),
+                    start=(block == 0),
+                    stop=(block == N_BLOCKS - 1),
+                )
+            z_sb = work.tile([P, PIECE], BF16, name="z_sb")
+            nc.vector.tensor_copy(z_sb[:], z_ps[:])
+
+            logstd_ps = banks.tile([P, PIECE], F32, name="logstd_ps", tag="bank")
+            for block in range(N_BLOCKS):
+                nc.tensor.matmul(
+                    logstd_ps[:],
+                    tmsT_sb[:, block, H2 : 2 * H2],
+                    adj(block, piece),
+                    start=(block == 0),
+                    stop=(block == N_BLOCKS - 1),
+                )
+            mean_ps = banks.tile([P, PIECE], F32, name="mean_ps", tag="bank")
+            nc.tensor.matmul(mean_ps[:], wp_sb[:], z_sb[:], start=True, stop=True)
+
+            std_sb = work.tile([P, PIECE], F32, name="std_sb")
+            nc.scalar.activation(std_sb[:], logstd_ps[:], FUNC.Exp)
+            spread_sb = work.tile([P, PIECE], F32, name="spread_sb")
+            nc.vector.tensor_mul(spread_sb[:], std_sb[:], noise_sb[:, cols])
+            out_sb = work.tile([P, PIECE], F32, name="out_sb")
+            nc.vector.scalar_tensor_tensor(
+                out_sb[:], mean_ps[:], bp_sb[:, 0:1], spread_sb[:], ALU.add, ALU.add
+            )
+            nc.sync.dma_start(out[:, cols], out_sb[:])

@@ -16,6 +16,15 @@ BLOCKS_PER_PIECE = PIECE // P
 H1_HALVES = H1 // P
 OFFSET_COLS = PIECE // 16
 
+OUT_RANGES = [(piece * PIECE, PIECE) for piece in range(N_PIECES - 1)] + [
+    (N - PIECE, PIECE // 2),
+    (N - PIECE // 2, PIECE // 2),
+]
+LATE_BLOCKS = range(N_BLOCKS - BLOCKS_PER_PIECE, N_BLOCKS)
+EARLY_BLOCKS = range(0, N_BLOCKS - BLOCKS_PER_PIECE)
+
+WARM_UP_MATMULS = 12
+
 FLOPS = 2 * (P * H1 * N + H1 * N * N + 2 * H1 * H2 * N + 2 * H2 * N * N + H2 * H2 * N)
 
 
@@ -25,41 +34,58 @@ def tile_vgae_encoder_b_kernel(tc, table, w1, adj_t, wm, ws, wp, bp, noise, offs
         tc.tile_pool(name="held", bufs=1) as held,
         tc.tile_pool(name="work", bufs=2) as work,
         tc.psum_pool(name="banks", bufs=4) as banks,
-        tc.psum_pool(name="flipped", bufs=2) as flipped,
-        tc.psum_pool(name="projected", bufs=2) as projected,
+        tc.psum_pool(name="turned", bufs=4) as turned,
     ):
+        zeros_sb = held.tile([P, PIECE], BF16, name="zeros_sb")
+        nc.vector.memset(zeros_sb[:], 0.0)
+        unused_ps = banks.tile([P, PIECE], F32, name="unused_ps", tag="bank")
+        for repeat in range(WARM_UP_MATMULS):
+            nc.tensor.matmul(unused_ps[:], zeros_sb[:, 0:P], zeros_sb[:], start=True, stop=True)
+
         offsets = held.tile([P, N // 16], U16, name="offsets")
         nc.sync.dma_start(offsets[:], offs)
-        table_sb = held.tile([P, S], BF16, name="table_sb")
-        nc.sync.dma_start(table_sb[:], table)
         w1_sb = held.tile([P, H1], BF16, name="w1_sb")
         nc.scalar.dma_start(w1_sb[:], w1)
+        table_sb = held.tile([P, S], BF16, name="table_sb")
+        nc.sync.dma_start(table_sb[:, 0 : S // 2], table[:, 0 : S // 2])
+        nc.scalar.dma_start(table_sb[:, S // 2 : S], table[:, S // 2 : S])
 
         adj_blocks = adj_t.rearrange("(b p) i -> p b i", p=P)
-        adj_sb = []
-        for piece in range(N_PIECES):
-            cols = slice(piece * PIECE, (piece + 1) * PIECE)
-            row = []
+        adj_sb = [
+            [
+                held.tile([P, BLOCKS_PER_PIECE, PIECE], BF16, name=f"adj_{piece}_{g}")
+                for g in range(N_BLOCKS // BLOCKS_PER_PIECE)
+            ]
+            for piece in range(N_PIECES)
+        ]
+
+        def load_adj(piece):
             for g in range(N_BLOCKS // BLOCKS_PER_PIECE):
-                part = held.tile([P, BLOCKS_PER_PIECE, PIECE], BF16, name=f"adj_{piece}_{g}")
                 nc.sync.dma_start(
-                    part[:], adj_blocks[:, g * BLOCKS_PER_PIECE : (g + 1) * BLOCKS_PER_PIECE, cols]
+                    adj_sb[piece][g][:],
+                    adj_blocks[
+                        :,
+                        g * BLOCKS_PER_PIECE : (g + 1) * BLOCKS_PER_PIECE,
+                        piece * PIECE : (piece + 1) * PIECE,
+                    ],
                 )
-                row.append(part)
-            adj_sb.append(row)
-            if piece == 0:
-                wms_sb = held.tile([P, H1_HALVES, 2 * H2], BF16, name="wms_sb")
-                nc.sync.dma_start(wms_sb[:, :, 0:H2], wm.rearrange("(h p) c -> p h c", p=P))
-                nc.sync.dma_start(wms_sb[:, :, H2 : 2 * H2], ws.rearrange("(h p) c -> p h c", p=P))
-                wp_sb = held.tile([P, H2], BF16, name="wp_sb")
-                nc.sync.dma_start(wp_sb[:], wp)
-                bp_sb = held.tile([P, 1], F32, name="bp_sb")
-                nc.sync.dma_start(bp_sb[:], bp)
+
+        def adj(block, first, width):
+            part = adj_sb[first // PIECE][block // BLOCKS_PER_PIECE]
+            return part[:, block % BLOCKS_PER_PIECE, first % PIECE : first % PIECE + width]
+
+        load_adj(0)
+        wms_sb = held.tile([P, H1_HALVES, 2 * H2], BF16, name="wms_sb")
+        nc.sync.dma_start(wms_sb[:, :, 0:H2], wm.rearrange("(h p) c -> p h c", p=P))
+        nc.sync.dma_start(wms_sb[:, :, H2 : 2 * H2], ws.rearrange("(h p) c -> p h c", p=P))
+        wp_sb = held.tile([P, H2], BF16, name="wp_sb")
+        nc.sync.dma_start(wp_sb[:], wp)
+        bp_sb = held.tile([P, 1], F32, name="bp_sb")
+        nc.sync.dma_start(bp_sb[:], bp)
+        for piece in range(1, N_PIECES):
+            load_adj(piece)
         noise_sb = held.tile([P, N], F32, name="noise_sb")
         nc.sync.dma_start(noise_sb[:], noise)
-
-        def adj(block, piece):
-            return adj_sb[piece][block // BLOCKS_PER_PIECE][:, block % BLOCKS_PER_PIECE, :]
 
         identity = held.tile([P, P], BF16, name="identity")
         make_identity(nc, identity[:])
@@ -84,7 +110,7 @@ def tile_vgae_encoder_b_kernel(tc, table, w1, adj_t, wm, ws, wp, bp, noise, offs
 
         xwT_sb = held.tile([P, N_BLOCKS, H1], BF16, name="xwT_sb")
         for piece in range(N_PIECES):
-            xwT_ps = flipped.tile([P, BLOCKS_PER_PIECE, H1], BF16, name="xwT_ps")
+            xwT_ps = turned.tile([P, BLOCKS_PER_PIECE, H1], BF16, name="xwT_ps", tag="turned")
             for k in range(BLOCKS_PER_PIECE):
                 block = piece * BLOCKS_PER_PIECE + k
                 for h in range(H1_HALVES):
@@ -93,72 +119,86 @@ def tile_vgae_encoder_b_kernel(tc, table, w1, adj_t, wm, ws, wp, bp, noise, offs
                         xw_sb[h][:, block * P : (block + 1) * P],
                         identity[:],
                     )
-            nc.vector.tensor_copy(
-                xwT_sb[:, piece * BLOCKS_PER_PIECE : (piece + 1) * BLOCKS_PER_PIECE, :], xwT_ps[:]
-            )
+            piece_blocks = slice(piece * BLOCKS_PER_PIECE, (piece + 1) * BLOCKS_PER_PIECE)
+            if piece % 2 == 0:
+                nc.vector.tensor_copy(xwT_sb[:, piece_blocks, :], xwT_ps[:])
+            else:
+                nc.scalar.activation(xwT_sb[:, piece_blocks, :], xwT_ps[:], FUNC.Copy)
 
         hidden_sb = [held.tile([P, N], BF16, name=f"hidden_sb{h}") for h in range(H1_HALVES)]
         tmsT_sb = held.tile([P, N_BLOCKS, 2 * H2], BF16, name="tmsT_sb")
-        for piece in range(N_PIECES):
+
+        def hidden_half(piece, h):
             cols = slice(piece * PIECE, (piece + 1) * PIECE)
-            for h in range(H1_HALVES):
-                hidden_ps = banks.tile([P, PIECE], F32, name="hidden_ps", tag="bank")
-                for block in range(N_BLOCKS):
-                    nc.tensor.matmul(
-                        hidden_ps[:],
-                        xwT_sb[:, block, h * P : (h + 1) * P],
-                        adj(block, piece),
-                        start=(block == 0),
-                        stop=(block == N_BLOCKS - 1),
-                    )
-                if h == 0:
-                    nc.scalar.activation(hidden_sb[h][:, cols], hidden_ps[:], FUNC.Relu)
+            hidden_ps = banks.tile([P, PIECE], F32, name="hidden_ps", tag="bank")
+            for block in range(N_BLOCKS):
+                nc.tensor.matmul(
+                    hidden_ps[:],
+                    xwT_sb[:, block, h * P : (h + 1) * P],
+                    adj(block, piece * PIECE, PIECE),
+                    start=(block == 0),
+                    stop=(block == N_BLOCKS - 1),
+                )
+            if h == 0:
+                nc.scalar.activation(hidden_sb[h][:, cols], hidden_ps[:], FUNC.Relu)
+            else:
+                nc.vector.tensor_scalar_max(hidden_sb[h][:, cols], hidden_ps[:], 0.0)
+
+        def project(piece):
+            for pair in range(BLOCKS_PER_PIECE // 2):
+                first_block = piece * BLOCKS_PER_PIECE + 2 * pair
+                tmsT_ps = turned.tile([P, 2, 2 * H2], F32, name="tmsT_ps", tag="turned")
+                for k in range(2):
+                    block = first_block + k
+                    for h in range(H1_HALVES):
+                        nc.tensor.matmul(
+                            tmsT_ps[:, k, :],
+                            hidden_sb[h][:, block * P : (block + 1) * P],
+                            wms_sb[:, h, :],
+                            start=(h == 0),
+                            stop=(h == H1_HALVES - 1),
+                        )
+                if pair == 0:
+                    nc.scalar.activation(tmsT_sb[:, first_block : first_block + 2, :], tmsT_ps[:], FUNC.Copy)
                 else:
-                    nc.vector.tensor_scalar_max(hidden_sb[h][:, cols], hidden_ps[:], 0.0)
-            for k in range(BLOCKS_PER_PIECE):
-                block = piece * BLOCKS_PER_PIECE + k
-                tmsT_ps = projected.tile([P, 2 * H2], F32, name="tmsT_ps")
-                for h in range(H1_HALVES):
-                    nc.tensor.matmul(
-                        tmsT_ps[:],
-                        hidden_sb[h][:, block * P : (block + 1) * P],
-                        wms_sb[:, h, :],
-                        start=(h == 0),
-                        stop=(h == H1_HALVES - 1),
-                    )
-                nc.vector.tensor_copy(tmsT_sb[:, block, :], tmsT_ps[:])
+                    nc.vector.tensor_copy(tmsT_sb[:, first_block : first_block + 2, :], tmsT_ps[:])
 
         for piece in range(N_PIECES):
-            cols = slice(piece * PIECE, (piece + 1) * PIECE)
-            z_ps = banks.tile([P, PIECE], F32, name="z_ps", tag="bank")
-            for block in range(N_BLOCKS):
-                nc.tensor.matmul(
-                    z_ps[:],
-                    tmsT_sb[:, block, 0:H2],
-                    adj(block, piece),
-                    start=(block == 0),
-                    stop=(block == N_BLOCKS - 1),
-                )
-            z_sb = work.tile([P, PIECE], BF16, name="z_sb")
-            nc.vector.tensor_copy(z_sb[:], z_ps[:])
+            hidden_half(piece, 0)
+            if piece > 0:
+                project(piece - 1)
+            hidden_half(piece, 1)
 
-            logstd_ps = banks.tile([P, PIECE], F32, name="logstd_ps", tag="bank")
-            for block in range(N_BLOCKS):
+        def contract(acc_ps, first_c, first, width, blocks):
+            for block in blocks:
                 nc.tensor.matmul(
-                    logstd_ps[:],
-                    tmsT_sb[:, block, H2 : 2 * H2],
-                    adj(block, piece),
+                    acc_ps[:],
+                    tmsT_sb[:, block, first_c : first_c + H2],
+                    adj(block, first, width),
                     start=(block == 0),
                     stop=(block == N_BLOCKS - 1),
                 )
-            mean_ps = banks.tile([P, PIECE], F32, name="mean_ps", tag="bank")
+
+        for first, width in OUT_RANGES:
+            cols = slice(first, first + width)
+            z_ps = banks.tile([P, width], F32, name="z_ps", tag="bank")
+            logstd_ps = banks.tile([P, width], F32, name="logstd_ps", tag="bank")
+            contract(z_ps, 0, first, width, EARLY_BLOCKS)
+            if first == 0:
+                project(N_PIECES - 1)
+            contract(logstd_ps, H2, first, width, EARLY_BLOCKS)
+            contract(z_ps, 0, first, width, LATE_BLOCKS)
+            z_sb = work.tile([P, width], BF16, name="z_sb", tag="z_sb")
+            nc.vector.tensor_copy(z_sb[:], z_ps[:])
+            contract(logstd_ps, H2, first, width, LATE_BLOCKS)
+            mean_ps = banks.tile([P, width], F32, name="mean_ps", tag="bank")
             nc.tensor.matmul(mean_ps[:], wp_sb[:], z_sb[:], start=True, stop=True)
 
-            std_sb = work.tile([P, PIECE], F32, name="std_sb")
+            std_sb = work.tile([P, width], F32, name="std_sb", tag="std_sb")
             nc.scalar.activation(std_sb[:], logstd_ps[:], FUNC.Exp)
-            spread_sb = work.tile([P, PIECE], F32, name="spread_sb")
+            spread_sb = work.tile([P, width], F32, name="spread_sb", tag="spread_sb")
             nc.vector.tensor_mul(spread_sb[:], std_sb[:], noise_sb[:, cols])
-            out_sb = work.tile([P, PIECE], F32, name="out_sb")
+            out_sb = work.tile([P, width], F32, name="out_sb", tag="out_sb")
             nc.vector.scalar_tensor_tensor(
                 out_sb[:], mean_ps[:], bp_sb[:, 0:1], spread_sb[:], ALU.add, ALU.add
             )

@@ -114,10 +114,12 @@ def tile_vgae_encoder_b_kernel(tc, table, w1, adj_t, wm, ws, wp, bp, noise, offs
             for k in range(BLOCKS_PER_PIECE):
                 block = piece * BLOCKS_PER_PIECE + k
                 for h in range(H1_HALVES):
-                    nc.tensor.transpose(
+                    nc.tensor.matmul(
                         xwT_ps[:, k, h * P : (h + 1) * P],
                         xw_sb[h][:, block * P : (block + 1) * P],
                         identity[:],
+                        start=True,
+                        stop=True,
                     )
             piece_blocks = slice(piece * BLOCKS_PER_PIECE, (piece + 1) * BLOCKS_PER_PIECE)
             if piece % 2 == 0:

@@ -23,8 +23,6 @@ OUT_RANGES = [(piece * PIECE, PIECE) for piece in range(N_PIECES - 1)] + [
 LATE_BLOCKS = range(N_BLOCKS - BLOCKS_PER_PIECE, N_BLOCKS)
 EARLY_BLOCKS = range(0, N_BLOCKS - BLOCKS_PER_PIECE)
 
-WARM_UP_MATMULS = 12
-
 FLOPS = 2 * (P * H1 * N + H1 * N * N + 2 * H1 * H2 * N + 2 * H2 * N * N + H2 * H2 * N)
 
 
@@ -36,12 +34,6 @@ def tile_vgae_encoder_b_kernel(tc, table, w1, adj_t, wm, ws, wp, bp, noise, offs
         tc.psum_pool(name="banks", bufs=4) as banks,
         tc.psum_pool(name="turned", bufs=4) as turned,
     ):
-        zeros_sb = held.tile([P, PIECE], BF16, name="zeros_sb")
-        nc.vector.memset(zeros_sb[:], 0.0)
-        unused_ps = banks.tile([P, PIECE], F32, name="unused_ps", tag="bank")
-        for repeat in range(WARM_UP_MATMULS):
-            nc.tensor.matmul(unused_ps[:], zeros_sb[:, 0:P], zeros_sb[:], start=True, stop=True)
-
         offsets = held.tile([P, N // 16], U16, name="offsets")
         nc.sync.dma_start(offsets[:], offs)
         w1_sb = held.tile([P, H1], BF16, name="w1_sb")
@@ -114,12 +106,10 @@ def tile_vgae_encoder_b_kernel(tc, table, w1, adj_t, wm, ws, wp, bp, noise, offs
             for k in range(BLOCKS_PER_PIECE):
                 block = piece * BLOCKS_PER_PIECE + k
                 for h in range(H1_HALVES):
-                    nc.tensor.matmul(
+                    nc.tensor.transpose(
                         xwT_ps[:, k, h * P : (h + 1) * P],
                         xw_sb[h][:, block * P : (block + 1) * P],
                         identity[:],
-                        start=True,
-                        stop=True,
                     )
             piece_blocks = slice(piece * BLOCKS_PER_PIECE, (piece + 1) * BLOCKS_PER_PIECE)
             if piece % 2 == 0:

@@ -20,8 +20,6 @@ OUT_RANGES = [(piece * PIECE, PIECE) for piece in range(N_PIECES - 1)] + [
     (N - PIECE, PIECE // 2),
     (N - PIECE // 2, PIECE // 2),
 ]
-LATE_BLOCKS = range(N_BLOCKS - BLOCKS_PER_PIECE, N_BLOCKS)
-EARLY_BLOCKS = range(0, N_BLOCKS - BLOCKS_PER_PIECE)
 
 FLOPS = 2 * (P * H1 * N + H1 * N * N + 2 * H1 * H2 * N + 2 * H2 * N * N + H2 * H2 * N)
 
@@ -31,8 +29,7 @@ def tile_vgae_encoder_b_kernel(tc, table, w1, adj_t, wm, ws, wp, bp, noise, offs
     with (
         tc.tile_pool(name="held", bufs=1) as held,
         tc.tile_pool(name="work", bufs=2) as work,
-        tc.psum_pool(name="banks", bufs=4) as banks,
-        tc.psum_pool(name="turned", bufs=4) as turned,
+        tc.psum_pool(name="banks", bufs=8) as banks,
     ):
         offsets = held.tile([P, N // 16], U16, name="offsets")
         nc.sync.dma_start(offsets[:], offs)
@@ -102,7 +99,7 @@ def tile_vgae_encoder_b_kernel(tc, table, w1, adj_t, wm, ws, wp, bp, noise, offs
 
         xwT_sb = held.tile([P, N_BLOCKS, H1], BF16, name="xwT_sb")
         for piece in range(N_PIECES):
-            xwT_ps = turned.tile([P, BLOCKS_PER_PIECE, H1], BF16, name="xwT_ps", tag="turned")
+            xwT_ps = banks.tile([P, BLOCKS_PER_PIECE, H1], BF16, name="xwT_ps", tag="bank")
             for k in range(BLOCKS_PER_PIECE):
                 block = piece * BLOCKS_PER_PIECE + k
                 for h in range(H1_HALVES):
@@ -139,7 +136,7 @@ def tile_vgae_encoder_b_kernel(tc, table, w1, adj_t, wm, ws, wp, bp, noise, offs
         def project(piece):
             for pair in range(BLOCKS_PER_PIECE // 2):
                 first_block = piece * BLOCKS_PER_PIECE + 2 * pair
-                tmsT_ps = turned.tile([P, 2, 2 * H2], F32, name="tmsT_ps", tag="turned")
+                tmsT_ps = banks.tile([P, 2, 2 * H2], F32, name="tmsT_ps", tag="bank")
                 for k in range(2):
                     block = first_block + k
                     for h in range(H1_HALVES):
@@ -156,13 +153,12 @@ def tile_vgae_encoder_b_kernel(tc, table, w1, adj_t, wm, ws, wp, bp, noise, offs
                     nc.vector.tensor_copy(tmsT_sb[:, first_block : first_block + 2, :], tmsT_ps[:])
 
         for piece in range(N_PIECES):
-            hidden_half(piece, 0)
-            if piece > 0:
-                project(piece - 1)
-            hidden_half(piece, 1)
+            for h in range(H1_HALVES):
+                hidden_half(piece, h)
+            project(piece)
 
-        def contract(acc_ps, first_c, first, width, blocks):
-            for block in blocks:
+        def contract(acc_ps, first_c, first, width):
+            for block in range(N_BLOCKS):
                 nc.tensor.matmul(
                     acc_ps[:],
                     tmsT_sb[:, block, first_c : first_c + H2],
@@ -175,14 +171,10 @@ def tile_vgae_encoder_b_kernel(tc, table, w1, adj_t, wm, ws, wp, bp, noise, offs
             cols = slice(first, first + width)
             z_ps = banks.tile([P, width], F32, name="z_ps", tag="bank")
             logstd_ps = banks.tile([P, width], F32, name="logstd_ps", tag="bank")
-            contract(z_ps, 0, first, width, EARLY_BLOCKS)
-            if first == 0:
-                project(N_PIECES - 1)
-            contract(logstd_ps, H2, first, width, EARLY_BLOCKS)
-            contract(z_ps, 0, first, width, LATE_BLOCKS)
+            contract(z_ps, 0, first, width)
             z_sb = work.tile([P, width], BF16, name="z_sb", tag="z_sb")
             nc.vector.tensor_copy(z_sb[:], z_ps[:])
-            contract(logstd_ps, H2, first, width, LATE_BLOCKS)
+            contract(logstd_ps, H2, first, width)
             mean_ps = banks.tile([P, width], F32, name="mean_ps", tag="bank")
             nc.tensor.matmul(mean_ps[:], wp_sb[:], z_sb[:], start=True, stop=True)
 

@@ -80,39 +80,46 @@ def tile_vgae_encoder_b_kernel(tc, table, w1, adj_t, wm, ws, wp, bp, noise, offs
         make_identity(nc, identity[:])
 
         xw_sb = [held.tile([P, N], BF16, name=f"xw_sb{h}") for h in range(H1_HALVES)]
-        for piece in range(N_PIECES):
-            cols = slice(piece * PIECE, (piece + 1) * PIECE)
-            piece_offsets = offsets[:, piece * OFFSET_COLS : (piece + 1) * OFFSET_COLS]
-            for h in range(H1_HALVES):
-                xw_ps = banks.tile([P, PIECE], F32, name="xw_ps", tag="bank")
-                nc.tensor.matmul(
-                    xw_ps[:],
-                    w1_sb[:, h * P : (h + 1) * P],
-                    table_sb[:].indirect(piece_offsets),
-                    start=True,
-                    stop=True,
-                )
-                if h == 0:
-                    nc.scalar.activation(xw_sb[h][:, cols], xw_ps[:], FUNC.Copy)
-                else:
-                    nc.vector.tensor_copy(xw_sb[h][:, cols], xw_ps[:])
+        xwT_sb = [held.tile([P, N_BLOCKS, P], BF16, name=f"xwT_sb{h}") for h in range(H1_HALVES)]
+        xwT_ps = {}
 
-        xwT_sb = held.tile([P, N_BLOCKS, H1], BF16, name="xwT_sb")
-        for piece in range(N_PIECES):
-            xwT_ps = banks.tile([P, BLOCKS_PER_PIECE, H1], BF16, name="xwT_ps", tag="bank")
-            for k in range(BLOCKS_PER_PIECE):
-                block = piece * BLOCKS_PER_PIECE + k
-                for h in range(H1_HALVES):
-                    nc.tensor.transpose(
-                        xwT_ps[:, k, h * P : (h + 1) * P],
-                        xw_sb[h][:, block * P : (block + 1) * P],
-                        identity[:],
-                    )
-            piece_blocks = slice(piece * BLOCKS_PER_PIECE, (piece + 1) * BLOCKS_PER_PIECE)
-            if piece % 2 == 0:
-                nc.vector.tensor_copy(xwT_sb[:, piece_blocks, :], xwT_ps[:])
+        def copy_out(turn, dst, src):
+            if turn % 2 == 0:
+                nc.scalar.activation(dst, src, FUNC.Copy)
             else:
-                nc.scalar.activation(xwT_sb[:, piece_blocks, :], xwT_ps[:], FUNC.Copy)
+                nc.vector.tensor_copy(dst, src)
+
+        def gather(h, piece):
+            xw_ps = banks.tile([P, PIECE], F32, name="xw_ps", tag="bank")
+            nc.tensor.matmul(
+                xw_ps[:],
+                w1_sb[:, h * P : (h + 1) * P],
+                table_sb[:].indirect(offsets[:, piece * OFFSET_COLS : (piece + 1) * OFFSET_COLS]),
+                start=True,
+                stop=True,
+            )
+            copy_out(piece, xw_sb[h][:, piece * PIECE : (piece + 1) * PIECE], xw_ps[:])
+
+        def flip(h, block):
+            piece, k = divmod(block, BLOCKS_PER_PIECE)
+            if k == 0:
+                xwT_ps[(h, piece)] = banks.tile([P, BLOCKS_PER_PIECE, P], BF16, name="xwT_ps", tag="bank")
+            nc.tensor.transpose(
+                xwT_ps[(h, piece)][:, k, :], xw_sb[h][:, block * P : (block + 1) * P], identity[:]
+            )
+            if k == BLOCKS_PER_PIECE - 1:
+                copy_out(
+                    piece + 1,
+                    xwT_sb[h][:, piece * BLOCKS_PER_PIECE : (piece + 1) * BLOCKS_PER_PIECE, :],
+                    xwT_ps[(h, piece)][:],
+                )
+
+        for piece in range(N_PIECES):
+            gather(0, piece)
+        for piece in range(N_PIECES):
+            gather(1, piece)
+            for k in range(BLOCKS_PER_PIECE):
+                flip(0, piece * BLOCKS_PER_PIECE + k)
 
         hidden_sb = [held.tile([P, N], BF16, name=f"hidden_sb{h}") for h in range(H1_HALVES)]
         tmsT_sb = held.tile([P, N_BLOCKS, 2 * H2], BF16, name="tmsT_sb")
@@ -123,11 +130,13 @@ def tile_vgae_encoder_b_kernel(tc, table, w1, adj_t, wm, ws, wp, bp, noise, offs
             for block in range(N_BLOCKS):
                 nc.tensor.matmul(
                     hidden_ps[:],
-                    xwT_sb[:, block, h * P : (h + 1) * P],
+                    xwT_sb[h][:, block, :],
                     adj(block, piece * PIECE, PIECE),
                     start=(block == 0),
                     stop=(block == N_BLOCKS - 1),
                 )
+                if piece == 0 and h == 0:
+                    flip(1, block)
             if h == 0:
                 nc.scalar.activation(hidden_sb[h][:, cols], hidden_ps[:], FUNC.Relu)
             else:

@@ -18,7 +18,8 @@ OFFSET_COLS = PIECE // 16
 
 OUT_RANGES = [(piece * PIECE, PIECE) for piece in range(N_PIECES - 1)] + [
     (N - PIECE, PIECE // 2),
-    (N - PIECE // 2, PIECE // 2),
+    (N - PIECE // 2, PIECE // 4),
+    (N - PIECE // 4, PIECE // 4),
 ]
 
 FLOPS = 2 * (P * H1 * N + H1 * N * N + 2 * H1 * H2 * N + 2 * H2 * N * N + H2 * H2 * N)

@@ -16,10 +16,13 @@ BLOCKS_PER_PIECE = PIECE // P
 H1_HALVES = H1 // P
 OFFSET_COLS = PIECE // 16
 
-OUT_RANGES = [(piece * PIECE, PIECE) for piece in range(N_PIECES - 1)] + [
-    (N - PIECE, PIECE // 2),
-    (N - PIECE // 2, PIECE // 4),
-    (N - PIECE // 4, PIECE // 4),
+LOGSTD_RANGES = [[(piece * PIECE, PIECE)] for piece in range(N_PIECES - 1)] + [
+    [
+        (N - PIECE, PIECE // 2),
+        (N - PIECE // 2, PIECE // 4),
+        (N - PIECE // 4, PIECE // 8),
+        (N - PIECE // 8, PIECE // 8),
+    ]
 ]
 
 FLOPS = 2 * (P * H1 * N + H1 * N * N + 2 * H1 * H2 * N + 2 * H2 * N * N + H2 * H2 * N)
@@ -29,7 +32,7 @@ def tile_vgae_encoder_b_kernel(tc, table, w1, adj_t, wm, ws, wp, bp, noise, offs
     nc = tc.nc
     with (
         tc.tile_pool(name="held", bufs=1) as held,
-        tc.tile_pool(name="work", bufs=2) as work,
+        tc.tile_pool(name="work", bufs=4) as work,
         tc.psum_pool(name="banks", bufs=8) as banks,
     ):
         offsets = held.tile([P, N // 16], U16, name="offsets")
@@ -177,23 +180,30 @@ def tile_vgae_encoder_b_kernel(tc, table, w1, adj_t, wm, ws, wp, bp, noise, offs
                     stop=(block == N_BLOCKS - 1),
                 )
 
-        for first, width in OUT_RANGES:
-            cols = slice(first, first + width)
-            z_ps = banks.tile([P, width], F32, name="z_ps", tag="bank")
-            logstd_ps = banks.tile([P, width], F32, name="logstd_ps", tag="bank")
-            contract(z_ps, 0, first, width)
-            z_sb = work.tile([P, width], BF16, name="z_sb", tag="z_sb")
+        for piece in range(N_PIECES):
+            z_ps = banks.tile([P, PIECE], F32, name="z_ps", tag="bank")
+            contract(z_ps, 0, piece * PIECE, PIECE)
+            z_sb = work.tile([P, PIECE], BF16, name="z_sb", tag="z_sb")
             nc.vector.tensor_copy(z_sb[:], z_ps[:])
-            contract(logstd_ps, H2, first, width)
-            mean_ps = banks.tile([P, width], F32, name="mean_ps", tag="bank")
-            nc.tensor.matmul(mean_ps[:], wp_sb[:], z_sb[:], start=True, stop=True)
+            mean_ps = banks.tile([P, PIECE], F32, name="mean_ps", tag="bank")
+            for first, width in LOGSTD_RANGES[piece]:
+                cols = slice(first, first + width)
+                logstd_ps = banks.tile([P, width], F32, name="logstd_ps", tag="bank")
+                contract(logstd_ps, H2, first, width)
+                if first == piece * PIECE:
+                    nc.tensor.matmul(mean_ps[:], wp_sb[:], z_sb[:], start=True, stop=True)
 
-            std_sb = work.tile([P, width], F32, name="std_sb", tag="std_sb")
-            nc.scalar.activation(std_sb[:], logstd_ps[:], FUNC.Exp)
-            spread_sb = work.tile([P, width], F32, name="spread_sb", tag="spread_sb")
-            nc.vector.tensor_mul(spread_sb[:], std_sb[:], noise_sb[:, cols])
-            out_sb = work.tile([P, width], F32, name="out_sb", tag="out_sb")
-            nc.vector.scalar_tensor_tensor(
-                out_sb[:], mean_ps[:], bp_sb[:, 0:1], spread_sb[:], ALU.add, ALU.add
-            )
-            nc.sync.dma_start(out[:, cols], out_sb[:])
+                std_sb = work.tile([P, width], F32, name="std_sb", tag="std_sb")
+                nc.scalar.activation(std_sb[:], logstd_ps[:], FUNC.Exp)
+                spread_sb = work.tile([P, width], F32, name="spread_sb", tag="spread_sb")
+                nc.vector.tensor_mul(spread_sb[:], std_sb[:], noise_sb[:, cols])
+                out_sb = work.tile([P, width], F32, name="out_sb", tag="out_sb")
+                nc.vector.scalar_tensor_tensor(
+                    out_sb[:],
+                    mean_ps[:, first - piece * PIECE : first - piece * PIECE + width],
+                    bp_sb[:, 0:1],
+                    spread_sb[:],
+                    ALU.add,
+                    ALU.add,
+                )
+                nc.sync.dma_start(out[:, cols], out_sb[:])

@@ -15,6 +15,8 @@ N_BLOCKS = N // P
 BLOCKS_PER_PIECE = PIECE // P
 H1_HALVES = H1 // P
 OFFSET_COLS = PIECE // 16
+N_GATHERS = H1_HALVES * N_PIECES
+FLIP_LEAD = 6
 
 LOGSTD_RANGES = [[(piece * PIECE, PIECE)] for piece in range(N_PIECES - 1)] + [
     [
@@ -85,7 +87,6 @@ def tile_vgae_encoder_b_kernel(tc, table, w1, adj_t, wm, ws, wp, bp, noise, offs
 
         xw_sb = [held.tile([P, N], BF16, name=f"xw_sb{h}") for h in range(H1_HALVES)]
         xwT_sb = [held.tile([P, N_BLOCKS, P], BF16, name=f"xwT_sb{h}") for h in range(H1_HALVES)]
-        xwT_ps = {}
 
         def copy_out(turn, dst, src):
             if turn % 2 == 0:
@@ -104,26 +105,17 @@ def tile_vgae_encoder_b_kernel(tc, table, w1, adj_t, wm, ws, wp, bp, noise, offs
             )
             copy_out(piece, xw_sb[h][:, piece * PIECE : (piece + 1) * PIECE], xw_ps[:])
 
-        def flip(h, block):
-            piece, k = divmod(block, BLOCKS_PER_PIECE)
-            if k == 0:
-                xwT_ps[(h, piece)] = banks.tile([P, BLOCKS_PER_PIECE, P], BF16, name="xwT_ps", tag="bank")
-            nc.tensor.transpose(
-                xwT_ps[(h, piece)][:, k, :], xw_sb[h][:, block * P : (block + 1) * P], identity[:]
-            )
-            if k == BLOCKS_PER_PIECE - 1:
-                copy_out(
-                    piece + 1,
-                    xwT_sb[h][:, piece * BLOCKS_PER_PIECE : (piece + 1) * BLOCKS_PER_PIECE, :],
-                    xwT_ps[(h, piece)][:],
-                )
+        def flip(number):
+            h, block = divmod(number, N_BLOCKS)
+            xwT_ps = banks.tile([P, P], BF16, name="xwT_ps", tag="bank")
+            nc.tensor.transpose(xwT_ps[:], xw_sb[h][:, block * P : (block + 1) * P], identity[:])
+            copy_out(number, xwT_sb[h][:, block, :], xwT_ps[:])
 
-        for piece in range(N_PIECES):
-            gather(0, piece)
-        for piece in range(N_PIECES):
-            gather(1, piece)
-            for k in range(BLOCKS_PER_PIECE):
-                flip(0, piece * BLOCKS_PER_PIECE + k)
+        for h in range(H1_HALVES):
+            for piece in range(N_PIECES):
+                gather(h, piece)
+                if h * N_PIECES + piece >= N_GATHERS - FLIP_LEAD:
+                    flip(h * N_PIECES + piece - (N_GATHERS - FLIP_LEAD))
 
         hidden_sb = [held.tile([P, N], BF16, name=f"hidden_sb{h}") for h in range(H1_HALVES)]
         tmsT_sb = held.tile([P, N_BLOCKS, 2 * H2], BF16, name="tmsT_sb")
@@ -139,8 +131,9 @@ def tile_vgae_encoder_b_kernel(tc, table, w1, adj_t, wm, ws, wp, bp, noise, offs
                     start=(block == 0),
                     stop=(block == N_BLOCKS - 1),
                 )
-                if piece == 0 and h == 0:
-                    flip(1, block)
+                next_flip = h * N_BLOCKS + block + FLIP_LEAD
+                if piece == 0 and next_flip < H1_HALVES * N_BLOCKS:
+                    flip(next_flip)
             if h == 0:
                 nc.scalar.activation(hidden_sb[h][:, cols], hidden_ps[:], FUNC.Relu)
             else:

@@ -40,10 +40,9 @@ def tile_vgae_encoder_b_kernel(tc, table, w1, adj_t, wm, ws, wp, bp, noise, offs
         offsets = held.tile([P, N // 16], U16, name="offsets")
         nc.sync.dma_start(offsets[:], offs)
         w1_sb = held.tile([P, H1], BF16, name="w1_sb")
-        nc.scalar.dma_start(w1_sb[:], w1)
+        nc.sync.dma_start(w1_sb[:], w1)
         table_sb = held.tile([P, S], BF16, name="table_sb")
-        nc.sync.dma_start(table_sb[:, 0 : S // 2], table[:, 0 : S // 2])
-        nc.scalar.dma_start(table_sb[:, S // 2 : S], table[:, S // 2 : S])
+        nc.sync.dma_start(table_sb[:], table)
 
         adj_blocks = adj_t.rearrange("(b p) i -> p b i", p=P)
         adj_sb = [

@@ -37,12 +37,12 @@ def tile_vgae_encoder_b_kernel(tc, table, w1, adj_t, wm, ws, wp, bp, noise, offs
         tc.tile_pool(name="work", bufs=4) as work,
         tc.psum_pool(name="banks", bufs=8) as banks,
     ):
+        table_sb = held.tile([P, S], BF16, name="table_sb")
+        nc.sync.dma_start(table_sb[:], table)
         offsets = held.tile([P, N // 16], U16, name="offsets")
         nc.sync.dma_start(offsets[:], offs)
         w1_sb = held.tile([P, H1], BF16, name="w1_sb")
         nc.sync.dma_start(w1_sb[:], w1)
-        table_sb = held.tile([P, S], BF16, name="table_sb")
-        nc.sync.dma_start(table_sb[:], table)
 
         adj_blocks = adj_t.rearrange("(b p) i -> p b i", p=P)
         adj_sb = [

@@ -45,30 +45,20 @@ def tile_vgae_encoder_b_kernel(tc, table, w1, adj_t, wm, ws, wp, bp, noise, offs
         nc.sync.dma_start(w1_sb[:], w1)
 
         adj_blocks = adj_t.rearrange("(b p) i -> p b i", p=P)
-        adj_sb = [
-            [
-                held.tile([P, BLOCKS_PER_PIECE, PIECE], BF16, name=f"adj_{piece}_{g}")
-                for g in range(N_BLOCKS // BLOCKS_PER_PIECE)
-            ]
-            for piece in range(N_PIECES)
-        ]
+        adj_sb = [held.tile([P, N_BLOCKS, PIECE], BF16, name=f"adj_{piece}") for piece in range(N_PIECES)]
 
-        def load_adj(piece):
-            for g in range(N_BLOCKS // BLOCKS_PER_PIECE):
+        def load_adj(piece, n_dmas):
+            step = N_BLOCKS // n_dmas
+            for b in range(0, N_BLOCKS, step):
                 nc.sync.dma_start(
-                    adj_sb[piece][g][:],
-                    adj_blocks[
-                        :,
-                        g * BLOCKS_PER_PIECE : (g + 1) * BLOCKS_PER_PIECE,
-                        piece * PIECE : (piece + 1) * PIECE,
-                    ],
+                    adj_sb[piece][:, b : b + step, :],
+                    adj_blocks[:, b : b + step, piece * PIECE : (piece + 1) * PIECE],
                 )
 
         def adj(block, first, width):
-            part = adj_sb[first // PIECE][block // BLOCKS_PER_PIECE]
-            return part[:, block % BLOCKS_PER_PIECE, first % PIECE : first % PIECE + width]
+            return adj_sb[first // PIECE][:, block, first % PIECE : first % PIECE + width]
 
-        load_adj(0)
+        load_adj(0, 4)
         wms_sb = held.tile([P, H1_HALVES, 2 * H2], BF16, name="wms_sb")
         nc.sync.dma_start(wms_sb[:, :, 0:H2], wm.rearrange("(h p) c -> p h c", p=P))
         nc.sync.dma_start(wms_sb[:, :, H2 : 2 * H2], ws.rearrange("(h p) c -> p h c", p=P))
@@ -77,7 +67,7 @@ def tile_vgae_encoder_b_kernel(tc, table, w1, adj_t, wm, ws, wp, bp, noise, offs
         bp_sb = held.tile([P, 1], F32, name="bp_sb")
         nc.sync.dma_start(bp_sb[:], bp)
         for piece in range(1, N_PIECES):
-            load_adj(piece)
+            load_adj(piece, 1)
         noise_sb = held.tile([P, N], F32, name="noise_sb")
         nc.sync.dma_start(noise_sb[:], noise)
 

@@ -16,7 +16,7 @@ BLOCKS_PER_PIECE = PIECE // P
 H1_HALVES = H1 // P
 OFFSET_COLS = PIECE // 16
 N_GATHERS = H1_HALVES * N_PIECES
-FLIP_LEAD = 6
+FLIP_LEAD = 5
 
 LOGSTD_RANGES = [[(piece * PIECE, PIECE)] for piece in range(N_PIECES - 1)] + [
     [
@@ -77,12 +77,6 @@ def tile_vgae_encoder_b_kernel(tc, table, w1, adj_t, wm, ws, wp, bp, noise, offs
         xw_sb = [held.tile([P, N], BF16, name=f"xw_sb{h}") for h in range(H1_HALVES)]
         xwT_sb = [held.tile([P, N_BLOCKS, P], BF16, name=f"xwT_sb{h}") for h in range(H1_HALVES)]
 
-        def copy_out(turn, dst, src):
-            if turn % 2 == 0:
-                nc.scalar.activation(dst, src, FUNC.Copy)
-            else:
-                nc.vector.tensor_copy(dst, src)
-
         def gather(h, piece):
             xw_ps = banks.tile([P, PIECE], F32, name="xw_ps", tag="bank")
             nc.tensor.matmul(
@@ -92,13 +86,17 @@ def tile_vgae_encoder_b_kernel(tc, table, w1, adj_t, wm, ws, wp, bp, noise, offs
                 start=True,
                 stop=True,
             )
-            copy_out(piece, xw_sb[h][:, piece * PIECE : (piece + 1) * PIECE], xw_ps[:])
+            xw_cols = xw_sb[h][:, piece * PIECE : (piece + 1) * PIECE]
+            if h == 0:
+                nc.vector.tensor_copy(xw_cols, xw_ps[:])
+            else:
+                nc.scalar.activation(xw_cols, xw_ps[:], FUNC.Copy)
 
         def flip(number):
             h, block = divmod(number, N_BLOCKS)
             xwT_ps = banks.tile([P, P], BF16, name="xwT_ps", tag="bank")
             nc.tensor.transpose(xwT_ps[:], xw_sb[h][:, block * P : (block + 1) * P], identity[:])
-            copy_out(number, xwT_sb[h][:, block, :], xwT_ps[:])
+            nc.vector.tensor_copy(xwT_sb[h][:, block, :], xwT_ps[:])
 
         for h in range(H1_HALVES):
             for piece in range(N_PIECES):

@@ -105,7 +105,7 @@ def tile_vgae_encoder_b_kernel(tc, table, w1, adj_t, wm, ws, wp, bp, noise, offs
                     flip(h * N_PIECES + piece - (N_GATHERS - FLIP_LEAD))
 
         hidden_sb = [held.tile([P, N], BF16, name=f"hidden_sb{h}") for h in range(H1_HALVES)]
-        tmsT_sb = held.tile([P, N_BLOCKS, 2 * H2], BF16, name="tmsT_sb")
+        tmsT_sb = held.tile([P, 2, N_BLOCKS, H2], BF16, name="tmsT_sb")
 
         def hidden_half(piece, h):
             cols = slice(piece * PIECE, (piece + 1) * PIECE)
@@ -140,21 +140,23 @@ def tile_vgae_encoder_b_kernel(tc, table, w1, adj_t, wm, ws, wp, bp, noise, offs
                             start=(h == 0),
                             stop=(h == H1_HALVES - 1),
                         )
+                tmsT_cols = tmsT_sb[:, :, first_block : first_block + 2, :].rearrange("p t b c -> p b t c")
+                tmsT_pair = tmsT_ps[:].rearrange("p b (t c) -> p b t c", t=2)
                 if pair == 0:
-                    nc.scalar.activation(tmsT_sb[:, first_block : first_block + 2, :], tmsT_ps[:], FUNC.Copy)
+                    nc.scalar.activation(tmsT_cols, tmsT_pair, FUNC.Copy)
                 else:
-                    nc.vector.tensor_copy(tmsT_sb[:, first_block : first_block + 2, :], tmsT_ps[:])
+                    nc.vector.tensor_copy(tmsT_cols, tmsT_pair)
 
         for piece in range(N_PIECES):
             for h in range(H1_HALVES):
                 hidden_half(piece, h)
             project(piece)
 
-        def contract(acc_ps, first_c, first, width):
+        def contract(acc_ps, t, first, width):
             for block in range(N_BLOCKS):
                 nc.tensor.matmul(
                     acc_ps[:],
-                    tmsT_sb[:, block, first_c : first_c + H2],
+                    tmsT_sb[:, t, block, :],
                     adj(block, first, width),
                     start=(block == 0),
                     stop=(block == N_BLOCKS - 1),
@@ -169,7 +171,7 @@ def tile_vgae_encoder_b_kernel(tc, table, w1, adj_t, wm, ws, wp, bp, noise, offs
             for first, width in LOGSTD_RANGES[piece]:
                 cols = slice(first, first + width)
                 logstd_ps = banks.tile([P, width], F32, name="logstd_ps", tag="bank")
-                contract(logstd_ps, H2, first, width)
+                contract(logstd_ps, 1, first, width)
                 if first == piece * PIECE:
                     nc.tensor.matmul(mean_ps[:], wp_sb[:], z_sb[:], start=True, stop=True)
 

import concourse.mybir as mybir
from concourse.masks import make_identity

BF16, F32, U16 = mybir.dt.bfloat16, mybir.dt.float32, mybir.dt.uint16
FUNC = mybir.ActivationFunctionType
ALU = mybir.AluOpType

P = 128
S = 4096
N = 2048
H1, H2 = 256, 128
PIECE = 512
N_PIECES = N // PIECE
N_BLOCKS = N // P
BLOCKS_PER_PIECE = PIECE // P
H1_HALVES = H1 // P
OFFSET_COLS = PIECE // 16
N_GATHERS = H1_HALVES * N_PIECES
FLIP_LEAD = 5

LOGSTD_RANGES = [[(piece * PIECE, PIECE)] for piece in range(N_PIECES - 1)] + [
    [
        (N - PIECE, PIECE // 2),
        (N - PIECE // 2, PIECE // 4),
        (N - PIECE // 4, PIECE // 8),
        (N - PIECE // 8, PIECE // 8),
    ]
]

FLOPS = 2 * (P * H1 * N + H1 * N * N + 2 * H1 * H2 * N + 2 * H2 * N * N + H2 * H2 * N)


def tile_vgae_encoder_b_kernel(tc, table, w1, adj_t, wm, ws, wp, bp, noise, offs, out):
    nc = tc.nc
    with (
        tc.tile_pool(name="held", bufs=1) as held,
        tc.tile_pool(name="work", bufs=4) as work,
        tc.psum_pool(name="banks", bufs=8) as banks,
    ):
        table_sb = held.tile([P, S], BF16, name="table_sb")
        nc.sync.dma_start(table_sb[:], table)
        offsets = held.tile([P, N // 16], U16, name="offsets")
        nc.sync.dma_start(offsets[:], offs)
        w1_sb = held.tile([P, H1], BF16, name="w1_sb")
        nc.sync.dma_start(w1_sb[:], w1)

        adj_blocks = adj_t.rearrange("(b p) i -> p b i", p=P)
        adj_sb = [held.tile([P, N_BLOCKS, PIECE], BF16, name=f"adj_{piece}") for piece in range(N_PIECES)]

        def load_adj(piece, n_dmas):
            step = N_BLOCKS // n_dmas
            for b in range(0, N_BLOCKS, step):
                nc.sync.dma_start(
                    adj_sb[piece][:, b : b + step, :],
                    adj_blocks[:, b : b + step, piece * PIECE : (piece + 1) * PIECE],
                )

        def adj(block, first, width):
            return adj_sb[first // PIECE][:, block, first % PIECE : first % PIECE + width]

        load_adj(0, 4)
        wms_sb = held.tile([P, H1_HALVES, 2 * H2], BF16, name="wms_sb")
        nc.sync.dma_start(wms_sb[:, :, 0:H2], wm.rearrange("(h p) c -> p h c", p=P))
        nc.sync.dma_start(wms_sb[:, :, H2 : 2 * H2], ws.rearrange("(h p) c -> p h c", p=P))
        wp_sb = held.tile([P, H2], BF16, name="wp_sb")
        nc.sync.dma_start(wp_sb[:], wp)
        bp_sb = held.tile([P, 1], F32, name="bp_sb")
        nc.sync.dma_start(bp_sb[:], bp)
        for piece in range(1, N_PIECES):
            load_adj(piece, 1)
        noise_sb = held.tile([P, N], F32, name="noise_sb")
        nc.sync.dma_start(noise_sb[:], noise)

        identity = held.tile([P, P], BF16, name="identity")
        make_identity(nc, identity[:])

        xw_sb = [held.tile([P, N], BF16, name=f"xw_sb{h}") for h in range(H1_HALVES)]
        xwT_sb = [held.tile([P, N_BLOCKS, P], BF16, name=f"xwT_sb{h}") for h in range(H1_HALVES)]

        def gather(h, piece):
            xw_ps = banks.tile([P, PIECE], F32, name="xw_ps", tag="bank")
            nc.tensor.matmul(
                xw_ps[:],
                w1_sb[:, h * P : (h + 1) * P],
                table_sb[:].indirect(offsets[:, piece * OFFSET_COLS : (piece + 1) * OFFSET_COLS]),
                start=True,
                stop=True,
            )
            xw_cols = xw_sb[h][:, piece * PIECE : (piece + 1) * PIECE]
            if h == 0:
                nc.vector.tensor_copy(xw_cols, xw_ps[:])
            else:
                nc.scalar.activation(xw_cols, xw_ps[:], FUNC.Copy)

        def flip(number):
            h, block = divmod(number, N_BLOCKS)
            xwT_ps = banks.tile([P, P], BF16, name="xwT_ps", tag="bank")
            nc.tensor.transpose(xwT_ps[:], xw_sb[h][:, block * P : (block + 1) * P], identity[:])
            nc.vector.tensor_copy(xwT_sb[h][:, block, :], xwT_ps[:])

        for h in range(H1_HALVES):
            for piece in range(N_PIECES):
                gather(h, piece)
                if h * N_PIECES + piece >= N_GATHERS - FLIP_LEAD:
                    flip(h * N_PIECES + piece - (N_GATHERS - FLIP_LEAD))

        hidden_sb = [held.tile([P, N], BF16, name=f"hidden_sb{h}") for h in range(H1_HALVES)]
        tmsT_sb = held.tile([P, 2, N_BLOCKS, H2], BF16, name="tmsT_sb")

        def hidden_half(piece, h):
            cols = slice(piece * PIECE, (piece + 1) * PIECE)
            hidden_ps = banks.tile([P, PIECE], F32, name="hidden_ps", tag="bank")
            for block in range(N_BLOCKS):
                nc.tensor.matmul(
                    hidden_ps[:],
                    xwT_sb[h][:, block, :],
                    adj(block, piece * PIECE, PIECE),
                    start=(block == 0),
                    stop=(block == N_BLOCKS - 1),
                )
                next_flip = h * N_BLOCKS + block + FLIP_LEAD
                if piece == 0 and next_flip < H1_HALVES * N_BLOCKS:
                    flip(next_flip)
            if h == 0:
                nc.scalar.activation(hidden_sb[h][:, cols], hidden_ps[:], FUNC.Relu)
            else:
                nc.vector.tensor_scalar_max(hidden_sb[h][:, cols], hidden_ps[:], 0.0)

        def project(piece):
            for pair in range(BLOCKS_PER_PIECE // 2):
                first_block = piece * BLOCKS_PER_PIECE + 2 * pair
                tmsT_ps = banks.tile([P, 2, 2 * H2], F32, name="tmsT_ps", tag="bank")
                for k in range(2):
                    block = first_block + k
                    for h in range(H1_HALVES):
                        nc.tensor.matmul(
                            tmsT_ps[:, k, :],
                            hidden_sb[h][:, block * P : (block + 1) * P],
                            wms_sb[:, h, :],
                            start=(h == 0),
                            stop=(h == H1_HALVES - 1),
                        )
                tmsT_cols = tmsT_sb[:, :, first_block : first_block + 2, :].rearrange("p t b c -> p b t c")
                tmsT_pair = tmsT_ps[:].rearrange("p b (t c) -> p b t c", t=2)
                if pair == 0:
                    nc.scalar.activation(tmsT_cols, tmsT_pair, FUNC.Copy)
                else:
                    nc.vector.tensor_copy(tmsT_cols, tmsT_pair)

        for piece in range(N_PIECES):
            for h in range(H1_HALVES):
                hidden_half(piece, h)
            project(piece)

        def contract(acc_ps, t, first, width):
            for block in range(N_BLOCKS):
                nc.tensor.matmul(
                    acc_ps[:],
                    tmsT_sb[:, t, block, :],
                    adj(block, first, width),
                    start=(block == 0),
                    stop=(block == N_BLOCKS - 1),
                )

        for piece in range(N_PIECES):
            z_ps = banks.tile([P, PIECE], F32, name="z_ps", tag="bank")
            contract(z_ps, 0, piece * PIECE, PIECE)
            z_sb = work.tile([P, PIECE], BF16, name="z_sb", tag="z_sb")
            nc.vector.tensor_copy(z_sb[:], z_ps[:])
            mean_ps = banks.tile([P, PIECE], F32, name="mean_ps", tag="bank")
            for first, width in LOGSTD_RANGES[piece]:
                cols = slice(first, first + width)
                logstd_ps = banks.tile([P, width], F32, name="logstd_ps", tag="bank")
                contract(logstd_ps, 1, first, width)
                if first == piece * PIECE:
                    nc.tensor.matmul(mean_ps[:], wp_sb[:], z_sb[:], start=True, stop=True)

                std_sb = work.tile([P, width], F32, name="std_sb", tag="std_sb")
                nc.scalar.activation(std_sb[:], logstd_ps[:], FUNC.Exp)
                spread_sb = work.tile([P, width], F32, name="spread_sb", tag="spread_sb")
                nc.vector.tensor_mul(spread_sb[:], std_sb[:], noise_sb[:, cols])
                out_sb = work.tile([P, width], F32, name="out_sb", tag="out_sb")
                nc.vector.scalar_tensor_tensor(
                    out_sb[:],
                    mean_ps[:, first - piece * PIECE : first - piece * PIECE + width],
                    bp_sb[:, 0:1],
                    spread_sb[:],
                    ALU.add,
                    ALU.add,
                )
                nc.sync.dma_start(out[:, cols], out_sb[:])
